import numpy as np
import ml_dtypes


def mxq(x, axis, fmt="e4m3"):
    dtype, down = {"e4m3": (ml_dtypes.float8_e4m3fn, 7), "e5m2": (ml_dtypes.float8_e5m2, 14)}[fmt]
    v = np.moveaxis(np.asarray(x, np.float32).astype(ml_dtypes.bfloat16).astype(np.float64), axis, -1)
    blocks = v.reshape(v.shape[:-1] + (-1, 32))
    amax = np.abs(blocks).max(-1, keepdims=True)
    byte = np.maximum(np.where(amax > 0, np.frexp(amax)[1] - 1 + 127, 0) - down, 1)
    scale = np.exp2(byte - 127.0)
    codes = (blocks / scale).astype(np.float32).astype(dtype).astype(np.float64)
    return np.moveaxis((codes * scale).reshape(v.shape), -1, axis)


WIDE = False


def mx_kscale(k):
    if not WIDE:
        return np.ones(k)
    levels = np.array([20, -20, 10, -10, 0])
    a = np.random.permutation(np.resize(levels, k // 512 * 4)).reshape(k // 512, 4)
    idx = np.arange(k)
    return np.exp2(a[idx // 512, idx % 128 // 32])


BF16 = ml_dtypes.bfloat16


def bf(x):
    return np.asarray(x, np.float32).astype(BF16)


def f64(x):
    return np.asarray(x).astype(np.float64)


B, C, P, Q, R = 1024, 1024, 16, 16, 16
D = P * Q * R


def setup_inputs():
    s = mx_kscale(B)
    core = np.random.standard_normal((B, P, Q, R)) * s[:, None, None, None]
    weights = np.random.standard_normal((C, P, Q, R)) / np.sqrt(D)
    g = np.random.standard_normal((B, C)) * np.exp2(np.random.randint(-12, 1, (B, 1))) / s[:, None]
    return {"core": bf(core), "weights": bf(weights), "grad_out": bf(g)}


def reference(core, weights, grad_out):
    b = core.shape[0]
    x = mxq(f64(core).reshape(b, -1), 0, "e4m3")
    g = mxq(f64(grad_out), 0, "e5m2")
    return (g.T @ x).reshape(weights.shape)

@@ -1,0 +1,129 @@
+from contextlib import ExitStack
+
+import concourse.mybir as mybir
+
+BF16 = mybir.dt.bfloat16
+F32 = mybir.dt.float32
+U32 = mybir.dt.uint32
+U8 = mybir.dt.uint8
+E4M3X4 = mybir.dt.float8_e4m3fn_x4
+E5M2X4 = mybir.dt.float8_e5m2_x4
+
+P = 128
+PACK = 4
+PASSES = 2
+B = 1024
+C = 1024
+D = 4096
+N_TILE = 512
+JOB_W = 1024
+PAIRS = D // JOB_W
+M_TILES = C // P
+
+FLOPS = 2 * B * C * D
+BYTES = 2 * B * D + 2 * B * C + 4 * C * D
+
+STAGE_BUFS = 16
+V_CELLS = {0: (9, 11), 1: (9, 11), 2: (9, 11, 13, 15), 3: (1, 3, 5, 7, 9, 11, 13, 15)}
+
+
+def tile_tensoroutputlayer_kernel(tc, core, weights, grad_out, out):
+    nc = tc.nc
+    x_dram = core.rearrange("b i j k -> b (i j k)").rearrange(
+        "(c p t) w -> c p t w", c=PASSES, p=P, t=PACK
+    )
+    g_dram = grad_out.rearrange("(c p t) w -> c p t w", c=PASSES, p=P, t=PACK)
+    out_dram = out.rearrange("c i j k -> c (i j k)")
+
+    with ExitStack() as ctx:
+        raw = ctx.enter_context(tc.tile_pool(name="raw", bufs=1))
+        grp = ctx.enter_context(tc.tile_pool(name="grp", bufs=3))
+        keep = ctx.enter_context(tc.tile_pool(name="keep", bufs=1))
+        stage = ctx.enter_context(tc.tile_pool(name="stage", bufs=STAGE_BUFS))
+        psum = ctx.enter_context(tc.psum_pool(name="psum", bufs=8))
+
+        raws = {}
+        for c in range(PASSES):
+            t = raw.tile([P, PACK, JOB_W], BF16, name="g_raw%d" % c)
+            nc.sync.dma_start(out=t[:], in_=g_dram[c, :, :, :])
+            raws[("g", c)] = t
+        for q in range(PAIRS):
+            for c in range(PASSES):
+                t = raw.tile([P, PACK, JOB_W], BF16, name="x_raw%d_%d" % (q, c))
+                nc.sync.dma_start(
+                    out=t[:], in_=x_dram[c, :, :, q * JOB_W : (q + 1) * JOB_W]
+                )
+                raws[(q, c)] = t
+
+        grouped_of = {}
+        codes = {}
+        scales = {}
+
+        def regroup(copy, key, w0, w1):
+            copy(
+                out=grouped_of[key][:, w0:w1, :].rearrange("p (g i) t -> p g t i", i=4),
+                in_=raws[key][:, :, w0:w1].rearrange("p t (g i) -> p g t i", i=4),
+            )
+
+        def start_job(key, shared):
+            grouped_of[key] = grp.tile(
+                [P, JOB_W, PACK], BF16, name="grouped", tag="grouped", align_bytes=64
+            )
+            if shared:
+                regroup(nc.vector.tensor_copy, key, 0, JOB_W // 2)
+                regroup(nc.scalar.copy, key, JOB_W // 2, JOB_W)
+            else:
+                regroup(nc.vector.tensor_copy, key, 0, JOB_W)
+
+        def finish_job(key):
+            fmt = E5M2X4 if key[0] == "g" else E4M3X4
+            codes[key] = keep.tile(
+                [P, JOB_W], U32, name="codes_%s_%d" % key, align_bytes=64
+            )
+            scales[key] = keep.tile(
+                [P, JOB_W], U8, name="scales_%s_%d" % key, align_bytes=64
+            )
+            nc.vector.quantize_mx(
+                out=codes[key][:].bitcast(fmt),
+                scales=scales[key][:],
+                in_=grouped_of[key][:].rearrange("p w t -> p (w t)"),
+            )
+
+        start_job(("g", 0), True)
+        start_job(("g", 1), True)
+        finish_job(("g", 0))
+        start_job((0, 0), True)
+        finish_job(("g", 1))
+        start_job((0, 1), True)
+        finish_job((0, 0))
+        finish_job((0, 1))
+
+        for q in range(PAIRS):
+            if q + 1 < PAIRS:
+                start_job((q + 1, 0), False)
+                start_job((q + 1, 1), False)
+                finish_job((q + 1, 0))
+                finish_job((q + 1, 1))
+            for m in range(M_TILES):
+                st = stage.tile([P, JOB_W], F32, name="st", tag="st")
+                rows = slice(m * P, (m + 1) * P)
+                for h in range(2):
+                    cols = slice(h * N_TILE, (h + 1) * N_TILE)
+                    acc = psum.tile([P, N_TILE], F32, name="acc", tag="acc")
+                    for c in range(PASSES):
+                        nc.tensor.matmul_mx(
+                            out=acc[:],
+                            lhsT=codes[("g", c)][:, rows].bitcast(E5M2X4),
+                            lhsT_scale=scales[("g", c)][:, rows],
+                            rhs=codes[(q, c)][:, cols].bitcast(E4M3X4),
+                            rhs_scale=scales[(q, c)][:, cols],
+                            start=(c == 0),
+                            stop=(c == PASSES - 1),
+                        )
+                    if 2 * m + h in V_CELLS[q]:
+                        nc.vector.tensor_copy(out=st[:, cols], in_=acc[:])
+                    else:
+                        nc.scalar.copy(out=st[:, cols], in_=acc[:])
+                nc.sync.dma_start(
+                    out=out_dram[rows, q * JOB_W : (q + 1) * JOB_W], in_=st[:]
+                )

@@ -17,14 +17,10 @@ C = 1024
 D = 4096
 N_TILE = 512
 JOB_W = 1024
-PAIRS = D // JOB_W
 M_TILES = C // P
 
 FLOPS = 2 * B * C * D
 BYTES = 2 * B * D + 2 * B * C + 4 * C * D
-
-STAGE_BUFS = 16
-V_CELLS = {0: (9, 11), 1: (9, 11), 2: (9, 11, 13, 15), 3: (1, 3, 5, 7, 9, 11, 13, 15)}
 
 
 def tile_tensoroutputlayer_kernel(tc, core, weights, grad_out, out):
@@ -36,24 +32,30 @@ def tile_tensoroutputlayer_kernel(tc, core, weights, grad_out, out):
     out_dram = out.rearrange("c i j k -> c (i j k)")
 
     with ExitStack() as ctx:
+        big = ctx.enter_context(tc.tile_pool(name="big", bufs=6))
         raw = ctx.enter_context(tc.tile_pool(name="raw", bufs=1))
         grp = ctx.enter_context(tc.tile_pool(name="grp", bufs=3))
         keep = ctx.enter_context(tc.tile_pool(name="keep", bufs=1))
-        stage = ctx.enter_context(tc.tile_pool(name="stage", bufs=STAGE_BUFS))
+        stage = ctx.enter_context(tc.tile_pool(name="stage", bufs=12))
         psum = ctx.enter_context(tc.psum_pool(name="psum", bufs=8))
 
         raws = {}
         for c in range(PASSES):
-            t = raw.tile([P, PACK, JOB_W], BF16, name="g_raw%d" % c)
+            t = big.tile([P, PACK, JOB_W], BF16, name="g_raw", tag="big")
             nc.sync.dma_start(out=t[:], in_=g_dram[c, :, :, :])
-            raws[("g", c)] = t
-        for q in range(PAIRS):
+            raws[("g", c)] = t[:, :, :]
+        for q in range(2):
             for c in range(PASSES):
-                t = raw.tile([P, PACK, JOB_W], BF16, name="x_raw%d_%d" % (q, c))
+                t = big.tile([P, PACK, JOB_W], BF16, name="x_raw", tag="big")
                 nc.sync.dma_start(
                     out=t[:], in_=x_dram[c, :, :, q * JOB_W : (q + 1) * JOB_W]
                 )
-                raws[(q, c)] = t
+                raws[(q, c)] = t[:, :, :]
+        for c in range(PASSES):
+            t = raw.tile([P, PACK, 2 * JOB_W], BF16, name="x_raw_half%d" % c)
+            nc.sync.dma_start(out=t[:], in_=x_dram[c, :, :, 2 * JOB_W : 4 * JOB_W])
+            raws[(2, c)] = t[:, :, 0:JOB_W]
+            raws[(3, c)] = t[:, :, JOB_W : 2 * JOB_W]
 
         grouped_of = {}
         codes = {}
@@ -89,6 +91,26 @@ def tile_tensoroutputlayer_kernel(tc, core, weights, grad_out, out):
                 in_=grouped_of[key][:].rearrange("p w t -> p (w t)"),
             )
 
+        def cell(m, n, dst, on_vector):
+            rows = slice(m * P, (m + 1) * P)
+            q = n // 2
+            cols = slice((n % 2) * N_TILE, (n % 2 + 1) * N_TILE)
+            acc = psum.tile([P, N_TILE], F32, name="acc", tag="acc")
+            for c in range(PASSES):
+                nc.tensor.matmul_mx(
+                    out=acc[:],
+                    lhsT=codes[("g", c)][:, rows].bitcast(E5M2X4),
+                    lhsT_scale=scales[("g", c)][:, rows],
+                    rhs=codes[(q, c)][:, cols].bitcast(E4M3X4),
+                    rhs_scale=scales[(q, c)][:, cols],
+                    start=(c == 0),
+                    stop=(c == PASSES - 1),
+                )
+            if on_vector:
+                nc.vector.tensor_copy(out=dst, in_=acc[:])
+            else:
+                nc.scalar.copy(out=dst, in_=acc[:])
+
         start_job(("g", 0), True)
         start_job(("g", 1), True)
         finish_job(("g", 0))
@@ -98,32 +120,34 @@ def tile_tensoroutputlayer_kernel(tc, core, weights, grad_out, out):
         finish_job((0, 0))
         finish_job((0, 1))
 
-        for q in range(PAIRS):
-            if q + 1 < PAIRS:
-                start_job((q + 1, 0), False)
-                start_job((q + 1, 1), False)
-                finish_job((q + 1, 0))
-                finish_job((q + 1, 1))
+        for q in range(2):
+            if q == 0:
+                start_job((1, 0), False)
+                start_job((1, 1), False)
+                finish_job((1, 0))
+                start_job((2, 0), False)
+                finish_job((1, 1))
+            else:
+                start_job((3, 0), False)
+                finish_job((2, 0))
+                start_job((2, 1), False)
+                finish_job((3, 0))
+                start_job((3, 1), False)
+                finish_job((2, 1))
+                finish_job((3, 1))
             for m in range(M_TILES):
                 st = stage.tile([P, JOB_W], F32, name="st", tag="st")
-                rows = slice(m * P, (m + 1) * P)
                 for h in range(2):
-                    cols = slice(h * N_TILE, (h + 1) * N_TILE)
-                    acc = psum.tile([P, N_TILE], F32, name="acc", tag="acc")
-                    for c in range(PASSES):
-                        nc.tensor.matmul_mx(
-                            out=acc[:],
-                            lhsT=codes[("g", c)][:, rows].bitcast(E5M2X4),
-                            lhsT_scale=scales[("g", c)][:, rows],
-                            rhs=codes[(q, c)][:, cols].bitcast(E4M3X4),
-                            rhs_scale=scales[(q, c)][:, cols],
-                            start=(c == 0),
-                            stop=(c == PASSES - 1),
-                        )
-                    if 2 * m + h in V_CELLS[q]:
-                        nc.vector.tensor_copy(out=st[:, cols], in_=acc[:])
-                    else:
-                        nc.scalar.copy(out=st[:, cols], in_=acc[:])
+                    cell(m, 2 * q + h, st[:, h * N_TILE : (h + 1) * N_TILE], False)
                 nc.sync.dma_start(
-                    out=out_dram[rows, q * JOB_W : (q + 1) * JOB_W], in_=st[:]
+                    out=out_dram[m * P : (m + 1) * P, q * JOB_W : (q + 1) * JOB_W],
+                    in_=st[:],
                 )
+
+        for m in range(M_TILES):
+            wide = big.tile([P, 2 * JOB_W], F32, name="wide", tag="big")
+            for h in range(4):
+                cell(m, 4 + h, wide[:, h * N_TILE : (h + 1) * N_TILE], h % 2 == 1)
+            nc.sync.dma_start(
+                out=out_dram[m * P : (m + 1) * P, 2 * JOB_W : 4 * JOB_W], in_=wide[:]
+            )

@@ -22,6 +22,9 @@ M_TILES = C // P
 FLOPS = 2 * B * C * D
 BYTES = 2 * B * D + 2 * B * C + 4 * C * D
 
+AHEAD = 4
+V_CELLS_FIRST_HALF = (27, 29, 31)
+
 
 def tile_tensoroutputlayer_kernel(tc, core, weights, grad_out, out):
     nc = tc.nc
@@ -32,6 +35,7 @@ def tile_tensoroutputlayer_kernel(tc, core, weights, grad_out, out):
     out_dram = out.rearrange("c i j k -> c (i j k)")
 
     with ExitStack() as ctx:
+        ctx.enter_context(tc.manual_schedule())
         big = ctx.enter_context(tc.tile_pool(name="big", bufs=6))
         raw = ctx.enter_context(tc.tile_pool(name="raw", bufs=1))
         grp = ctx.enter_context(tc.tile_pool(name="grp", bufs=3))
@@ -40,26 +44,36 @@ def tile_tensoroutputlayer_kernel(tc, core, weights, grad_out, out):
         psum = ctx.enter_context(tc.psum_pool(name="psum", bufs=8))
 
         raws = {}
-        for c in range(PASSES):
-            t = big.tile([P, PACK, JOB_W], BF16, name="g_raw", tag="big")
-            nc.sync.dma_start(out=t[:], in_=g_dram[c, :, :, :])
-            raws[("g", c)] = t[:, :, :]
-        for q in range(2):
-            for c in range(PASSES):
-                t = big.tile([P, PACK, JOB_W], BF16, name="x_raw", tag="big")
-                nc.sync.dma_start(
-                    out=t[:], in_=x_dram[c, :, :, q * JOB_W : (q + 1) * JOB_W]
-                )
-                raws[(q, c)] = t[:, :, :]
-        for c in range(PASSES):
-            t = raw.tile([P, PACK, 2 * JOB_W], BF16, name="x_raw_half%d" % c)
-            nc.sync.dma_start(out=t[:], in_=x_dram[c, :, :, 2 * JOB_W : 4 * JOB_W])
-            raws[(2, c)] = t[:, :, 0:JOB_W]
-            raws[(3, c)] = t[:, :, JOB_W : 2 * JOB_W]
+
+        def load_narrow(key, src):
+            t = big.tile([P, PACK, JOB_W], BF16, name="narrow_raw", tag="big")
+            nc.sync.dma_start(out=t[:], in_=src)
+            raws[key] = t[:, :, :]
+
+        def load_wide(q, c):
+            t = raw.tile([P, PACK, 2 * JOB_W], BF16, name="wide_raw%d_%d" % (q, c))
+            nc.sync.dma_start(
+                out=t[:], in_=x_dram[c, :, :, q * JOB_W : (q + 2) * JOB_W]
+            )
+            raws[(q, c)] = t[:, :, 0:JOB_W]
+            raws[(q + 1, c)] = t[:, :, JOB_W : 2 * JOB_W]
+
+        load_narrow(("g", 0), g_dram[0, :, :, :])
+        load_narrow(("g", 1), g_dram[1, :, :, :])
+        load_wide(0, 0)
+        load_narrow((0, 1), x_dram[1, :, :, 0:JOB_W])
+        load_narrow((1, 1), x_dram[1, :, :, JOB_W : 2 * JOB_W])
+        load_wide(2, 0)
+        load_wide(2, 1)
 
         grouped_of = {}
         codes = {}
         scales = {}
+
+        def new_group(key):
+            grouped_of[key] = grp.tile(
+                [P, JOB_W, PACK], BF16, name="grouped", tag="grouped", align_bytes=64
+            )
 
         def regroup(copy, key, w0, w1):
             copy(
@@ -67,17 +81,13 @@ def tile_tensoroutputlayer_kernel(tc, core, weights, grad_out, out):
                 in_=raws[key][:, :, w0:w1].rearrange("p t (g i) -> p g t i", i=4),
             )
 
-        def start_job(key, shared):
-            grouped_of[key] = grp.tile(
-                [P, JOB_W, PACK], BF16, name="grouped", tag="grouped", align_bytes=64
-            )
-            if shared:
-                regroup(nc.vector.tensor_copy, key, 0, JOB_W // 2)
-                regroup(nc.scalar.copy, key, JOB_W // 2, JOB_W)
-            else:
-                regroup(nc.vector.tensor_copy, key, 0, JOB_W)
+        def on_vector(key, w0, w1):
+            regroup(nc.vector.tensor_copy, key, w0, w1)
 
-        def finish_job(key):
+        def on_scalar(key, w0, w1):
+            regroup(nc.scalar.copy, key, w0, w1)
+
+        def quantise(key):
             fmt = E5M2X4 if key[0] == "g" else E4M3X4
             codes[key] = keep.tile(
                 [P, JOB_W], U32, name="codes_%s_%d" % key, align_bytes=64
@@ -91,63 +101,102 @@ def tile_tensoroutputlayer_kernel(tc, core, weights, grad_out, out):
                 in_=grouped_of[key][:].rearrange("p w t -> p (w t)"),
             )
 
-        def cell(m, n, dst, on_vector):
+        def one_pass(acc, m, n, c):
             rows = slice(m * P, (m + 1) * P)
-            q = n // 2
             cols = slice((n % 2) * N_TILE, (n % 2 + 1) * N_TILE)
+            nc.tensor.matmul_mx(
+                out=acc[:],
+                lhsT=codes[("g", c)][:, rows].bitcast(E5M2X4),
+                lhsT_scale=scales[("g", c)][:, rows],
+                rhs=codes[(n // 2, c)][:, cols].bitcast(E4M3X4),
+                rhs_scale=scales[(n // 2, c)][:, cols],
+                start=(c == 0),
+                stop=(c == PASSES - 1),
+            )
+
+        def open_cell(m, n):
             acc = psum.tile([P, N_TILE], F32, name="acc", tag="acc")
-            for c in range(PASSES):
-                nc.tensor.matmul_mx(
-                    out=acc[:],
-                    lhsT=codes[("g", c)][:, rows].bitcast(E5M2X4),
-                    lhsT_scale=scales[("g", c)][:, rows],
-                    rhs=codes[(q, c)][:, cols].bitcast(E4M3X4),
-                    rhs_scale=scales[(q, c)][:, cols],
-                    start=(c == 0),
-                    stop=(c == PASSES - 1),
-                )
-            if on_vector:
+            one_pass(acc, m, n, 0)
+            return acc
+
+        def close_cell(acc, m, n, dst, vector_empties):
+            one_pass(acc, m, n, 1)
+            if vector_empties:
                 nc.vector.tensor_copy(out=dst, in_=acc[:])
             else:
                 nc.scalar.copy(out=dst, in_=acc[:])
 
-        start_job(("g", 0), True)
-        start_job(("g", 1), True)
-        finish_job(("g", 0))
-        start_job((0, 0), True)
-        finish_job(("g", 1))
-        start_job((0, 1), True)
-        finish_job((0, 0))
-        finish_job((0, 1))
+        half = JOB_W // 2
+        most = 3 * JOB_W // 4
 
-        for q in range(2):
-            if q == 0:
-                start_job((1, 0), False)
-                start_job((1, 1), False)
-                finish_job((1, 0))
-                start_job((2, 0), False)
-                finish_job((1, 1))
-            else:
-                start_job((3, 0), False)
-                finish_job((2, 0))
-                start_job((2, 1), False)
-                finish_job((3, 0))
-                start_job((3, 1), False)
-                finish_job((2, 1))
-                finish_job((3, 1))
-            for m in range(M_TILES):
+        for c in range(PASSES):
+            new_group(("g", c))
+            on_vector(("g", c), 0, half)
+            on_scalar(("g", c), half, JOB_W)
+        quantise(("g", 0))
+        quantise(("g", 1))
+        new_group((0, 0))
+        on_vector((0, 0), 0, half)
+        on_scalar((0, 0), half, JOB_W)
+        new_group((1, 0))
+        on_vector((1, 0), 0, half)
+        quantise((0, 0))
+        first_half = [(m, 2 * q + h) for q in range(2) for m in range(M_TILES) for h in range(2)]
+        ahead = [open_cell(m, n) for (m, n) in first_half[:AHEAD]]
+        new_group((0, 1))
+        on_vector((0, 1), 0, most)
+        on_scalar((0, 1), most, JOB_W)
+        on_scalar((1, 0), half, JOB_W)
+        quantise((0, 1))
+        new_group((1, 1))
+        on_vector((1, 1), 0, half)
+        on_scalar((1, 1), half, JOB_W)
+        quantise((1, 0))
+        quantise((1, 1))
+
+        new_group((2, 0))
+        on_vector((2, 0), 0, JOB_W)
+        new_group((3, 0))
+        on_vector((3, 0), 0, JOB_W)
+        quantise((2, 0))
+        new_group((2, 1))
+        on_vector((2, 1), 0, JOB_W)
+        quantise((3, 0))
+        new_group((3, 1))
+        on_vector((3, 1), 0, JOB_W)
+        quantise((2, 1))
+        quantise((3, 1))
+
+        st = None
+        for i, (m, n) in enumerate(first_half):
+            h = n % 2
+            if h == 0:
                 st = stage.tile([P, JOB_W], F32, name="st", tag="st")
-                for h in range(2):
-                    cell(m, 2 * q + h, st[:, h * N_TILE : (h + 1) * N_TILE], False)
+            acc = ahead[i] if i < AHEAD else open_cell(m, n)
+            close_cell(
+                acc, m, n, st[:, h * N_TILE : (h + 1) * N_TILE], i in V_CELLS_FIRST_HALF
+            )
+            if h == 1:
+                q = n // 2
                 nc.sync.dma_start(
                     out=out_dram[m * P : (m + 1) * P, q * JOB_W : (q + 1) * JOB_W],
                     in_=st[:],
                 )
 
-        for m in range(M_TILES):
+        for m in range(M_TILES - 1):
             wide = big.tile([P, 2 * JOB_W], F32, name="wide", tag="big")
             for h in range(4):
-                cell(m, 4 + h, wide[:, h * N_TILE : (h + 1) * N_TILE], h % 2 == 1)
+                acc = open_cell(m, 4 + h)
+                close_cell(acc, m, 4 + h, wide[:, h * N_TILE : (h + 1) * N_TILE], h % 2 == 1)
             nc.sync.dma_start(
                 out=out_dram[m * P : (m + 1) * P, 2 * JOB_W : 4 * JOB_W], in_=wide[:]
+            )
+        m = M_TILES - 1
+        for q in (2, 3):
+            st = stage.tile([P, JOB_W], F32, name="st", tag="st")
+            for h in range(2):
+                acc = open_cell(m, 2 * q + h)
+                close_cell(acc, m, 2 * q + h, st[:, h * N_TILE : (h + 1) * N_TILE], h == 1)
+            nc.sync.dma_start(
+                out=out_dram[m * P : (m + 1) * P, q * JOB_W : (q + 1) * JOB_W], in_=st[:]
             )

@@ -23,7 +23,7 @@ FLOPS = 2 * B * C * D
 BYTES = 2 * B * D + 2 * B * C + 4 * C * D
 
 AHEAD = 4
-V_CELLS_FIRST_HALF = (27, 29, 31)
+VECTOR_EMPTIES = (27, 29, 31)
 
 
 def tile_tensoroutputlayer_kernel(tc, core, weights, grad_out, out):
@@ -52,9 +52,7 @@ def tile_tensoroutputlayer_kernel(tc, core, weights, grad_out, out):
 
         def load_wide(q, c):
             t = raw.tile([P, PACK, 2 * JOB_W], BF16, name="wide_raw%d_%d" % (q, c))
-            nc.sync.dma_start(
-                out=t[:], in_=x_dram[c, :, :, q * JOB_W : (q + 2) * JOB_W]
-            )
+            nc.sync.dma_start(out=t[:], in_=x_dram[c, :, :, q * JOB_W : (q + 2) * JOB_W])
             raws[(q, c)] = t[:, :, 0:JOB_W]
             raws[(q + 1, c)] = t[:, :, JOB_W : 2 * JOB_W]
 
@@ -89,12 +87,8 @@ def tile_tensoroutputlayer_kernel(tc, core, weights, grad_out, out):
 
         def quantise(key):
             fmt = E5M2X4 if key[0] == "g" else E4M3X4
-            codes[key] = keep.tile(
-                [P, JOB_W], U32, name="codes_%s_%d" % key, align_bytes=64
-            )
-            scales[key] = keep.tile(
-                [P, JOB_W], U8, name="scales_%s_%d" % key, align_bytes=64
-            )
+            codes[key] = keep.tile([P, JOB_W], U32, name="codes_%s_%d" % key, align_bytes=64)
+            scales[key] = keep.tile([P, JOB_W], U8, name="scales_%s_%d" % key, align_bytes=64)
             nc.vector.quantize_mx(
                 out=codes[key][:].bitcast(fmt),
                 scales=scales[key][:],
@@ -128,7 +122,6 @@ def tile_tensoroutputlayer_kernel(tc, core, weights, grad_out, out):
 
         half = JOB_W // 2
         most = 3 * JOB_W // 4
-
         for c in range(PASSES):
             new_group(("g", c))
             on_vector(("g", c), 0, half)
@@ -154,18 +147,13 @@ def tile_tensoroutputlayer_kernel(tc, core, weights, grad_out, out):
         quantise((1, 0))
         quantise((1, 1))
 
-        new_group((2, 0))
-        on_vector((2, 0), 0, JOB_W)
-        new_group((3, 0))
-        on_vector((3, 0), 0, JOB_W)
-        quantise((2, 0))
-        new_group((2, 1))
-        on_vector((2, 1), 0, JOB_W)
-        quantise((3, 0))
-        new_group((3, 1))
-        on_vector((3, 1), 0, JOB_W)
-        quantise((2, 1))
-        quantise((3, 1))
+        late_jobs = [(2, 0), (3, 0), (2, 1), (3, 1)]
+        for k, key in enumerate(late_jobs):
+            new_group(key)
+            on_vector(key, 0, JOB_W)
+            if k > 0:
+                quantise(late_jobs[k - 1])
+        quantise(late_jobs[-1])
 
         st = None
         for i, (m, n) in enumerate(first_half):
@@ -173,30 +161,18 @@ def tile_tensoroutputlayer_kernel(tc, core, weights, grad_out, out):
             if h == 0:
                 st = stage.tile([P, JOB_W], F32, name="st", tag="st")
             acc = ahead[i] if i < AHEAD else open_cell(m, n)
-            close_cell(
-                acc, m, n, st[:, h * N_TILE : (h + 1) * N_TILE], i in V_CELLS_FIRST_HALF
-            )
+            close_cell(acc, m, n, st[:, h * N_TILE : (h + 1) * N_TILE], i in VECTOR_EMPTIES)
             if h == 1:
                 q = n // 2
                 nc.sync.dma_start(
-                    out=out_dram[m * P : (m + 1) * P, q * JOB_W : (q + 1) * JOB_W],
-                    in_=st[:],
+                    out=out_dram[m * P : (m + 1) * P, q * JOB_W : (q + 1) * JOB_W], in_=st[:]
                 )
 
-        for m in range(M_TILES - 1):
+        for m in range(M_TILES):
             wide = big.tile([P, 2 * JOB_W], F32, name="wide", tag="big")
             for h in range(4):
                 acc = open_cell(m, 4 + h)
                 close_cell(acc, m, 4 + h, wide[:, h * N_TILE : (h + 1) * N_TILE], h % 2 == 1)
             nc.sync.dma_start(
                 out=out_dram[m * P : (m + 1) * P, 2 * JOB_W : 4 * JOB_W], in_=wide[:]
-            )
-        m = M_TILES - 1
-        for q in (2, 3):
-            st = stage.tile([P, JOB_W], F32, name="st", tag="st")
-            for h in range(2):
-                acc = open_cell(m, 2 * q + h)
-                close_cell(acc, m, 2 * q + h, st[:, h * N_TILE : (h + 1) * N_TILE], h == 1)
-            nc.sync.dma_start(
-                out=out_dram[m * P : (m + 1) * P, q * JOB_W : (q + 1) * JOB_W], in_=st[:]
             )

from contextlib import ExitStack

import concourse.mybir as mybir

BF16 = mybir.dt.bfloat16
F32 = mybir.dt.float32
U32 = mybir.dt.uint32
U8 = mybir.dt.uint8
E4M3X4 = mybir.dt.float8_e4m3fn_x4
E5M2X4 = mybir.dt.float8_e5m2_x4

P = 128
PACK = 4
PASSES = 2
B = 1024
C = 1024
D = 4096
N_TILE = 512
JOB_W = 1024
M_TILES = C // P

FLOPS = 2 * B * C * D
BYTES = 2 * B * D + 2 * B * C + 4 * C * D

AHEAD = 4
VECTOR_EMPTIES = (27, 29, 31)


def tile_tensoroutputlayer_kernel(tc, core, weights, grad_out, out):
    nc = tc.nc
    x_dram = core.rearrange("b i j k -> b (i j k)").rearrange(
        "(c p t) w -> c p t w", c=PASSES, p=P, t=PACK
    )
    g_dram = grad_out.rearrange("(c p t) w -> c p t w", c=PASSES, p=P, t=PACK)
    out_dram = out.rearrange("c i j k -> c (i j k)")

    with ExitStack() as ctx:
        ctx.enter_context(tc.manual_schedule())
        big = ctx.enter_context(tc.tile_pool(name="big", bufs=6))
        raw = ctx.enter_context(tc.tile_pool(name="raw", bufs=1))
        grp = ctx.enter_context(tc.tile_pool(name="grp", bufs=3))
        keep = ctx.enter_context(tc.tile_pool(name="keep", bufs=1))
        stage = ctx.enter_context(tc.tile_pool(name="stage", bufs=12))
        psum = ctx.enter_context(tc.psum_pool(name="psum", bufs=8))

        raws = {}

        def load_narrow(key, src):
            t = big.tile([P, PACK, JOB_W], BF16, name="narrow_raw", tag="big")
            nc.sync.dma_start(out=t[:], in_=src)
            raws[key] = t[:, :, :]

        def load_wide(q, c):
            t = raw.tile([P, PACK, 2 * JOB_W], BF16, name="wide_raw%d_%d" % (q, c))
            nc.sync.dma_start(out=t[:], in_=x_dram[c, :, :, q * JOB_W : (q + 2) * JOB_W])
            raws[(q, c)] = t[:, :, 0:JOB_W]
            raws[(q + 1, c)] = t[:, :, JOB_W : 2 * JOB_W]

        load_narrow(("g", 0), g_dram[0, :, :, :])
        load_narrow(("g", 1), g_dram[1, :, :, :])
        load_wide(0, 0)
        load_narrow((0, 1), x_dram[1, :, :, 0:JOB_W])
        load_narrow((1, 1), x_dram[1, :, :, JOB_W : 2 * JOB_W])
        load_wide(2, 0)
        load_wide(2, 1)

        grouped_of = {}
        codes = {}
        scales = {}

        def new_group(key):
            grouped_of[key] = grp.tile(
                [P, JOB_W, PACK], BF16, name="grouped", tag="grouped", align_bytes=64
            )

        def regroup(copy, key, w0, w1):
            copy(
                out=grouped_of[key][:, w0:w1, :].rearrange("p (g i) t -> p g t i", i=4),
                in_=raws[key][:, :, w0:w1].rearrange("p t (g i) -> p g t i", i=4),
            )

        def on_vector(key, w0, w1):
            regroup(nc.vector.tensor_copy, key, w0, w1)

        def on_scalar(key, w0, w1):
            regroup(nc.scalar.copy, key, w0, w1)

        def quantise(key):
            fmt = E5M2X4 if key[0] == "g" else E4M3X4
            codes[key] = keep.tile([P, JOB_W], U32, name="codes_%s_%d" % key, align_bytes=64)
            scales[key] = keep.tile([P, JOB_W], U8, name="scales_%s_%d" % key, align_bytes=64)
            nc.vector.quantize_mx(
                out=codes[key][:].bitcast(fmt),
                scales=scales[key][:],
                in_=grouped_of[key][:].rearrange("p w t -> p (w t)"),
            )

        def one_pass(acc, m, n, c):
            rows = slice(m * P, (m + 1) * P)
            cols = slice((n % 2) * N_TILE, (n % 2 + 1) * N_TILE)
            nc.tensor.matmul_mx(
                out=acc[:],
                lhsT=codes[("g", c)][:, rows].bitcast(E5M2X4),
                lhsT_scale=scales[("g", c)][:, rows],
                rhs=codes[(n // 2, c)][:, cols].bitcast(E4M3X4),
                rhs_scale=scales[(n // 2, c)][:, cols],
                start=(c == 0),
                stop=(c == PASSES - 1),
            )

        def open_cell(m, n):
            acc = psum.tile([P, N_TILE], F32, name="acc", tag="acc")
            one_pass(acc, m, n, 0)
            return acc

        def close_cell(acc, m, n, dst, vector_empties):
            one_pass(acc, m, n, 1)
            if vector_empties:
                nc.vector.tensor_copy(out=dst, in_=acc[:])
            else:
                nc.scalar.copy(out=dst, in_=acc[:])

        half = JOB_W // 2
        most = 3 * JOB_W // 4
        for c in range(PASSES):
            new_group(("g", c))
            on_vector(("g", c), 0, half)
            on_scalar(("g", c), half, JOB_W)
        quantise(("g", 0))
        quantise(("g", 1))
        new_group((0, 0))
        on_vector((0, 0), 0, half)
        on_scalar((0, 0), half, JOB_W)
        new_group((1, 0))
        on_vector((1, 0), 0, half)
        quantise((0, 0))
        first_half = [(m, 2 * q + h) for q in range(2) for m in range(M_TILES) for h in range(2)]
        ahead = [open_cell(m, n) for (m, n) in first_half[:AHEAD]]
        new_group((0, 1))
        on_vector((0, 1), 0, most)
        on_scalar((0, 1), most, JOB_W)
        on_scalar((1, 0), half, JOB_W)
        quantise((0, 1))
        new_group((1, 1))
        on_vector((1, 1), 0, half)
        on_scalar((1, 1), half, JOB_W)
        quantise((1, 0))
        quantise((1, 1))

        late_jobs = [(2, 0), (3, 0), (2, 1), (3, 1)]
        for k, key in enumerate(late_jobs):
            new_group(key)
            on_vector(key, 0, JOB_W)
            if k > 0:
                quantise(late_jobs[k - 1])
        quantise(late_jobs[-1])

        st = None
        for i, (m, n) in enumerate(first_half):
            h = n % 2
            if h == 0:
                st = stage.tile([P, JOB_W], F32, name="st", tag="st")
            acc = ahead[i] if i < AHEAD else open_cell(m, n)
            close_cell(acc, m, n, st[:, h * N_TILE : (h + 1) * N_TILE], i in VECTOR_EMPTIES)
            if h == 1:
                q = n // 2
                nc.sync.dma_start(
                    out=out_dram[m * P : (m + 1) * P, q * JOB_W : (q + 1) * JOB_W], in_=st[:]
                )

        for m in range(M_TILES):
            wide = big.tile([P, 2 * JOB_W], F32, name="wide", tag="big")
            for h in range(4):
                acc = open_cell(m, 4 + h)
                close_cell(acc, m, 4 + h, wide[:, h * N_TILE : (h + 1) * N_TILE], h % 2 == 1)
            nc.sync.dma_start(
                out=out_dram[m * P : (m + 1) * P, 2 * JOB_W : 4 * JOB_W], in_=wide[:]
            )
